import numpy as np
import ml_dtypes


def mxq(x, axis, fmt="e4m3"):
    dtype, down = {"e4m3": (ml_dtypes.float8_e4m3fn, 7), "e5m2": (ml_dtypes.float8_e5m2, 14)}[fmt]
    v = np.moveaxis(np.asarray(x, np.float32).astype(ml_dtypes.bfloat16).astype(np.float64), axis, -1)
    blocks = v.reshape(v.shape[:-1] + (-1, 32))
    amax = np.abs(blocks).max(-1, keepdims=True)
    byte = np.maximum(np.where(amax > 0, np.frexp(amax)[1] - 1 + 127, 0) - down, 1)
    scale = np.exp2(byte - 127.0)
    codes = (blocks / scale).astype(np.float32).astype(dtype).astype(np.float64)
    return np.moveaxis((codes * scale).reshape(v.shape), -1, axis)


WIDE = False


def mx_kscale(k):
    if not WIDE:
        return np.ones(k)
    levels = np.array([10, -10, 5, -5, 0])
    a = np.random.permutation(np.resize(levels, k // 512 * 4)).reshape(k // 512, 4)
    idx = np.arange(k)
    return np.exp2(a[idx // 512, idx % 128 // 32])


BF16 = ml_dtypes.bfloat16


def bf(x):
    return np.asarray(x, np.float32).astype(BF16)


def f64(x):
    return np.asarray(x).astype(np.float64)


E2M1 = np.array([0.0, 0.5, 1.0, 1.5, 2.0, 3.0, 4.0, 6.0, -0.0, -0.5, -1.0, -1.5, -2.0, -3.0, -4.0, -6.0])


def pack_weight(w, fmt):
    k, n = w.shape
    w = f64(bf(w)).reshape(k // 32, 32, n)
    amax = np.abs(w).max(1)
    if fmt == "e4m3":
        byte = np.frexp(amax)[1] - 1 + 127 - 7
    else:
        mant, ex = np.frexp(amax / 6.0)
        byte = np.where(mant > 0.5, ex, ex - 1) + 127
    byte = np.clip(np.where(amax > 0, byte, 1), 1, 254)
    scaled = (w * np.exp2(127.0 - byte)[:, None, :]).reshape(k, n).astype(np.float32)
    by_word = np.ascontiguousarray(scaled.reshape(k // 512, 128, 4, n).transpose(0, 1, 3, 2))
    if fmt == "e4m3":
        words = by_word.astype(ml_dtypes.float8_e4m3fn).view(np.uint8)
    else:
        c = by_word.astype(ml_dtypes.float4_e2m1fn).view(np.uint8) & 0xF
        words = c[..., 0::2] | (c[..., 1::2] << 4)
    return np.ascontiguousarray(words), np.ascontiguousarray(byte.astype(np.uint8).reshape(k // 512, 16, n))


def unpack_weight(words, scales, fmt):
    g, p, n, _ = words.shape
    if fmt == "e4m3":
        vals = np.ascontiguousarray(words).view(ml_dtypes.float8_e4m3fn).astype(np.float64)
    else:
        nib = np.empty((g, p, n, 4), np.uint8)
        nib[..., 0::2] = words & 0xF
        nib[..., 1::2] = words >> 4
        vals = E2M1[nib]
    vals = vals * np.repeat(np.exp2(scales.astype(np.float64) - 127.0), 8, axis=1)[..., None]
    return vals.transpose(0, 1, 3, 2).reshape(g * 512, n)


B, T, D, H, HD, F = 2, 64, 8192, 16, 64, 4096
A = H * HD
HH = HD // 2
EPS = 1e-5
ROPE_BASE = 10000.0
FMT = "e4m3"


def layernorm(x, g, b):
    mu = np.mean(x, axis=-1, keepdims=True)
    var = np.mean(np.square(x - mu), axis=-1, keepdims=True)
    return (x - mu) / np.sqrt(var + EPS) * g + b


def apply_rope(x, cos, sin):
    x1, x2 = x[..., :HH], x[..., HH:]
    cos = cos[None, None]
    sin = sin[None, None]
    return np.concatenate([x1 * cos - x2 * sin, x1 * sin + x2 * cos], axis=-1)


def setup_inputs():
    s = mx_kscale(D)
    ang = np.arange(T)[:, None] / ROPE_BASE ** (np.arange(HH) / HH)[None, :]
    x = bf(np.random.standard_normal((B, T, D)) + 0.5 * np.random.standard_normal((B, T, 1)))
    ln1_g = bf((1.0 + 0.1 * np.random.standard_normal(D)) * s)
    ln1_b = bf(0.1 * np.random.standard_normal(D) * s)
    words, scales = pack_weight(np.random.standard_normal((D, 3 * A)) / np.sqrt(D) / s[:, None], FMT)
    b_qkv = bf(0.1 * np.random.standard_normal(3 * A))
    return {"x": x,
            "rope_cos": bf(np.cos(ang)), "rope_sin": bf(np.sin(ang)),
            "ln1_g": ln1_g,
            "ln1_b": ln1_b,
            "w_qkv_words": words, "w_qkv_scales": scales,
            "b_qkv": b_qkv}


def reference(x, rope_cos, rope_sin, ln1_g, ln1_b, w_qkv_words, w_qkv_scales, b_qkv):
    h = layernorm(f64(x), f64(ln1_g), f64(ln1_b))
    qkv = ((mxq(h, 2, "e4m3") @ unpack_weight(w_qkv_words, w_qkv_scales, FMT)) + f64(b_qkv)).reshape(B, T, 3, H, HD)
    q, k, v = np.transpose(qkv, (2, 0, 3, 1, 4))
    q = apply_rope(q, f64(rope_cos), f64(rope_sin))
    k = apply_rope(k, f64(rope_cos), f64(rope_sin))
    return q, k, v

@@ -1,0 +1,251 @@
+from contextlib import ExitStack
+
+import concourse.mybir as mybir
+from concourse.masks import make_identity
+
+F32 = mybir.dt.float32
+BF16 = mybir.dt.bfloat16
+I32 = mybir.dt.int32
+U8 = mybir.dt.uint8
+FP8X4 = mybir.dt.float8_e4m3fn_x4
+ALU = mybir.AluOpType
+ACT = mybir.ActivationFunctionType
+
+P = 128
+PACK = 4
+K_PASS = P * PACK
+D = 8192
+GROUPS = D // K_PASS
+BANK = 512
+T = 64
+HD = 64
+HALF = HD // 2
+HEADS_PER_BANK = BANK // HD
+QK_COLS = 2048
+V_COLS = 1024
+N_ALL = QK_COLS + V_COLS
+QK_BANKS = QK_COLS // BANK
+V_BANKS = V_COLS // BANK
+X_CHUNK_GROUPS = 4
+X_CHUNK = X_CHUNK_GROUPS * K_PASS
+X_CHUNKS = D // X_CHUNK
+PLANES_PER_TILE = 4
+EPS = 1e-5
+
+FLOPS = 2 * P * D * N_ALL
+
+
+def tile_transformerblock_pa_k_kernel(
+    tc, x, rope_cos, rope_sin, ln1_g, ln1_b, w_qkv_words, w_qkv_scales, b_qkv, out_0, out_1, out_2
+):
+    nc = tc.nc
+    x_rows = x.rearrange("b t d -> (b t) d")
+
+    with ExitStack() as ctx:
+        keep = ctx.enter_context(tc.tile_pool(name="keep", bufs=1))
+        stage = ctx.enter_context(tc.tile_pool(name="stage", bufs=2))
+        weights = ctx.enter_context(tc.tile_pool(name="weights", bufs=12))
+        finish = ctx.enter_context(tc.tile_pool(name="finish", bufs=2))
+        psum_acc = ctx.enter_context(tc.psum_pool(name="psum_acc", bufs=1))
+        psum_work = ctx.enter_context(tc.psum_pool(name="psum_work", bufs=2))
+
+        gain_rows = keep.tile([P, K_PASS], BF16)
+        nc.vector.memset(gain_rows[:], 0.0)
+        nc.scalar.dma_start(out=gain_rows[0:GROUPS, :], in_=ln1_g.rearrange("(g k) -> g k", k=K_PASS))
+        nc.scalar.dma_start(
+            out=gain_rows[GROUPS : 2 * GROUPS, :], in_=ln1_b.rearrange("(g k) -> g k", k=K_PASS)
+        )
+        bias_row = keep.tile([P, N_ALL], BF16)
+        nc.vector.memset(bias_row[:], 0.0)
+        nc.scalar.dma_start(out=bias_row[0:1, :], in_=b_qkv.rearrange("(o n) -> o n", o=1))
+        rope_raw = keep.tile([P, 2, HALF], BF16)
+        for b in range(2):
+            nc.scalar.dma_start(out=rope_raw[b * T : (b + 1) * T, 0, :], in_=rope_cos)
+            nc.scalar.dma_start(out=rope_raw[b * T : (b + 1) * T, 1, :], in_=rope_sin)
+
+        x_chunks = []
+        for c in range(X_CHUNKS):
+            x_chunk = keep.tile([P, X_CHUNK], BF16, name="x_chunk%d" % c)
+            nc.sync.dma_start(out=x_chunk[:], in_=x_rows[:, c * X_CHUNK : (c + 1) * X_CHUNK])
+            x_chunks.append(x_chunk)
+
+        w_planes = keep.tile([P, GROUPS // PLANES_PER_TILE, N_ALL], U8, align_bytes=64)
+        nc.vector.memset(w_planes[:].bitcast(I32), 0)
+        for s in range(GROUPS // PLANES_PER_TILE):
+            for quadrant in range(4):
+                nc.sync.dma_start(
+                    out=w_planes[32 * quadrant : 32 * quadrant + 16, s, :].bitcast(I32),
+                    in_=w_qkv_scales[
+                        PLANES_PER_TILE * s : PLANES_PER_TILE * (s + 1),
+                        4 * quadrant : 4 * quadrant + 4,
+                        :,
+                    ].bitcast(I32),
+                )
+
+        ident = keep.tile([P, P], F32)
+        make_identity(nc, ident[:])
+        ones = keep.tile([P, P], BF16)
+        nc.vector.memset(ones[:], 1.0)
+        eps = keep.tile([P, 1], F32)
+        nc.vector.memset(eps[:], EPS)
+        table_warm = keep.tile([P, 1], F32)
+        nc.scalar.activation(out=table_warm[:], in_=eps[:], func=ACT.Sqrt)
+
+        bias_all = keep.tile([P, N_ALL], F32)
+        for j in range(N_ALL // BANK):
+            cols = slice(j * BANK, (j + 1) * BANK)
+            spread = psum_work.tile([P, BANK], F32, tag="work")
+            nc.tensor.matmul(out=spread[:], lhsT=ones[:], rhs=bias_row[:, cols], start=True, stop=True)
+            nc.scalar.copy(out=bias_all[:, cols], in_=spread[:])
+
+        gain_sorted = keep.tile([P, PACK, P], F32)
+        nc.vector.tensor_copy(out=gain_sorted[:], in_=gain_rows[:].rearrange("r (p t) -> r t p", t=PACK))
+        gain_t = psum_work.tile([P, PACK, P], F32, tag="work")
+        for t in range(PACK):
+            nc.tensor.transpose(gain_t[:, t, :], gain_sorted[:, t, :], ident[:])
+        gain_cols = keep.tile([P, PACK, 2 * GROUPS], F32)
+        nc.scalar.copy(out=gain_cols[:], in_=gain_t[:, :, 0 : 2 * GROUPS])
+
+        stats = keep.tile([P, GROUPS, 6], F32)
+        for g in range(GROUPS):
+            c, i = divmod(g, X_CHUNK_GROUPS)
+            nc.vector.bn_stats(out=stats[:, g, :], in_=x_chunks[c][:, i * K_PASS : (i + 1) * K_PASS])
+        mean_var = keep.tile([P, 2], F32)
+        nc.vector.bn_aggr(out=mean_var[:], in_=stats[:].rearrange("p g s -> p (g s)"))
+        std = keep.tile([P, 1], F32)
+        nc.scalar.activation(out=std[:], in_=mean_var[:, 1:2], func=ACT.Sqrt, bias=eps[:], scale=1.0)
+        rstd = keep.tile([P, 1], F32)
+        nc.vector.reciprocal(out=rstd[:], in_=std[:])
+
+        h_codes = keep.tile([P, GROUPS * P], I32, align_bytes=64)
+        h_planes = keep.tile([P, GROUPS * P], U8, align_bytes=64)
+        acc = [psum_acc.tile([P, BANK], F32, name="acc%d" % j) for j in range(QK_BANKS + V_BANKS)]
+
+        def normalise(c):
+            normed = stage.tile([P, X_CHUNK_GROUPS, PACK, P], F32, bufs=3)
+            nc.vector.tensor_scalar(
+                out=normed[:],
+                in0=x_chunks[c][:].rearrange("r (g p t) -> r g t p", g=X_CHUNK_GROUPS, t=PACK),
+                scalar1=mean_var[:, 0:1],
+                scalar2=rstd[:],
+                op0=ALU.subtract,
+                op1=ALU.mult,
+            )
+            return normed
+
+        def flip(c, normed):
+            h_by_t = stage.tile([P, X_CHUNK_GROUPS, PACK, P], BF16)
+            for i in range(X_CHUNK_GROUPS):
+                g = c * X_CHUNK_GROUPS + i
+                flipped = psum_work.tile([P, PACK, P], F32, tag="work")
+                for t in range(PACK):
+                    nc.tensor.transpose(flipped[:, t, :], normed[:, i, t, :], ident[:])
+                for t in range(PACK):
+                    nc.scalar.activation(
+                        out=h_by_t[:, i, t, :],
+                        in_=flipped[:, t, :],
+                        func=ACT.Identity,
+                        scale=gain_cols[:, t, g : g + 1],
+                        bias=gain_cols[:, t, GROUPS + g : GROUPS + g + 1],
+                    )
+            return h_by_t
+
+        def quantise(c, h_by_t):
+            grouped = stage.tile([P, X_CHUNK_GROUPS, P, PACK], BF16, align_bytes=64)
+            nc.vector.tensor_copy(out=grouped[:], in_=h_by_t[:].rearrange("p g t r -> p g r t"))
+            words = slice(c * X_CHUNK_GROUPS * P, (c + 1) * X_CHUNK_GROUPS * P)
+            nc.vector.quantize_mx(
+                out=h_codes[:, words].bitcast(FP8X4),
+                scales=h_planes[:, words],
+                in_=grouped[:].rearrange("p g r t -> p (g r t)"),
+            )
+
+        def project(g, first_col, n_cols):
+            w_words = weights.tile([P, n_cols], I32, tag="w", align_bytes=64)
+            nc.sync.dma_start(
+                out=w_words[:],
+                in_=w_qkv_words[g]
+                .rearrange("p n t -> p (n t)")[:, first_col * PACK : (first_col + n_cols) * PACK]
+                .bitcast(I32),
+            )
+            s, plane = divmod(g, PLANES_PER_TILE)
+            for j in range(n_cols // BANK):
+                bank = first_col // BANK + j
+                nc.tensor.matmul_mx(
+                    out=acc[bank][:],
+                    lhsT=h_codes[:, g * P : (g + 1) * P].bitcast(FP8X4),
+                    lhsT_scale=h_planes[:, g * P : (g + 1) * P],
+                    rhs=w_words[:, j * BANK : (j + 1) * BANK].bitcast(FP8X4),
+                    rhs_scale=w_planes[4 * plane : P, s, bank * BANK : (bank + 1) * BANK],
+                    start=(g == 0),
+                    stop=(g == GROUPS - 1),
+                )
+
+        def store(result, out_tensor, first_head, queue):
+            for b in range(2):
+                queue.dma_start(
+                    out=out_tensor[b, first_head : first_head + HEADS_PER_BANK].rearrange("h t d -> t h d"),
+                    in_=result[b * T : (b + 1) * T, :].rearrange("t (h d) -> t h d", d=HD),
+                )
+
+        normed_of = {}
+        h_by_t_of = {}
+        for step in range(X_CHUNKS + 2):
+            if step < X_CHUNKS:
+                normed_of[step] = normalise(step)
+            if 1 <= step <= X_CHUNKS:
+                h_by_t_of[step - 1] = flip(step - 1, normed_of[step - 1])
+            if step >= 2:
+                c = step - 2
+                quantise(c, h_by_t_of[c])
+                for g in range(c * X_CHUNK_GROUPS, (c + 1) * X_CHUNK_GROUPS):
+                    project(g, 0, QK_COLS)
+
+        cos_cos = keep.tile([P, 2, HALF], F32)
+        nc.vector.tensor_copy(out=cos_cos[:], in_=rope_raw[:, 0:1, :].to_broadcast([P, 2, HALF]))
+        sin_sin = keep.tile([P, 2, HALF], F32)
+        nc.vector.tensor_scalar(
+            out=sin_sin[:, 0, :], in0=rope_raw[:, 1, :], scalar1=-1.0, scalar2=None, op0=ALU.mult
+        )
+        nc.vector.tensor_copy(out=sin_sin[:, 1, :], in_=rope_raw[:, 1, :])
+
+        for bank in range(QK_BANKS):
+            cols = slice(bank * BANK, (bank + 1) * BANK)
+            biased = finish.tile([P, HEADS_PER_BANK, 2, HALF], F32)
+            nc.vector.tensor_tensor(
+                out=biased[:].rearrange("p h s d -> p (h s d)"), in0=acc[bank][:], in1=bias_all[:, cols], op=ALU.add
+            )
+            straight = finish.tile([P, HEADS_PER_BANK, 2, HALF], F32)
+            nc.vector.tensor_tensor(
+                out=straight[:].rearrange("p h s d -> p h (s d)"),
+                in0=biased[:].rearrange("p h s d -> p h (s d)"),
+                in1=cos_cos[:].rearrange("p s d -> p (s d)").unsqueeze(1).to_broadcast([P, HEADS_PER_BANK, HD]),
+                op=ALU.mult,
+            )
+            crossed = finish.tile([P, HEADS_PER_BANK, 2, HALF], F32)
+            for half in range(2):
+                nc.vector.tensor_tensor(
+                    out=crossed[:, :, half, :],
+                    in0=biased[:, :, 1 - half, :],
+                    in1=sin_sin[:, half : half + 1, :].to_broadcast([P, HEADS_PER_BANK, HALF]),
+                    op=ALU.mult,
+                )
+            rotated = finish.tile([P, BANK], F32)
+            nc.vector.tensor_tensor(
+                out=rotated[:],
+                in0=straight[:].rearrange("p h s d -> p (h s d)"),
+                in1=crossed[:].rearrange("p h s d -> p (h s d)"),
+                op=ALU.add,
+            )
+            out_tensor = out_0 if bank < QK_BANKS // 2 else out_1
+            store(rotated, out_tensor, (bank % 2) * HEADS_PER_BANK, nc.scalar)
+
+        for g in range(GROUPS):
+            project(g, QK_COLS, V_COLS)
+        for j in range(V_BANKS):
+            bank = QK_BANKS + j
+            value = finish.tile([P, BANK], F32)
+            nc.vector.tensor_tensor(
+                out=value[:], in0=acc[bank][:], in1=bias_all[:, bank * BANK : (bank + 1) * BANK], op=ALU.add
+            )
+            store(value, out_2, j * HEADS_PER_BANK, nc.sync)

@@ -73,13 +73,13 @@ def tile_transformerblock_pa_k_kernel(
         nc.vector.memset(w_planes[:].bitcast(I32), 0)
         for s in range(GROUPS // PLANES_PER_TILE):
             for quadrant in range(4):
-                nc.sync.dma_start(
-                    out=w_planes[32 * quadrant : 32 * quadrant + 16, s, :].bitcast(I32),
+                nc.gpsimd.dma_start(
+                    out=w_planes[32 * quadrant : 32 * quadrant + 16, s, :].bitcast(F32),
                     in_=w_qkv_scales[
                         PLANES_PER_TILE * s : PLANES_PER_TILE * (s + 1),
                         4 * quadrant : 4 * quadrant + 4,
                         :,
-                    ].bitcast(I32),
+                    ].bitcast(F32),
                 )
 
         ident = keep.tile([P, P], F32)

@@ -48,6 +48,7 @@ def tile_transformerblock_pa_k_kernel(
         finish = ctx.enter_context(tc.tile_pool(name="finish", bufs=2))
         psum_acc = ctx.enter_context(tc.psum_pool(name="psum_acc", bufs=1))
         psum_work = ctx.enter_context(tc.psum_pool(name="psum_work", bufs=2))
+        ctx.enter_context(tc.manual_schedule())
 
         gain_rows = keep.tile([P, K_PASS], BF16)
         nc.vector.memset(gain_rows[:], 0.0)
@@ -181,9 +182,9 @@ def tile_transformerblock_pa_k_kernel(
                     stop=(g == GROUPS - 1),
                 )
 
-        def store(result, out_tensor, first_head, queue):
+        def store(result, out_tensor, first_head):
             for b in range(2):
-                queue.dma_start(
+                nc.sync.dma_start(
                     out=out_tensor[b, first_head : first_head + HEADS_PER_BANK].rearrange("h t d -> t h d"),
                     in_=result[b * T : (b + 1) * T, :].rearrange("t (h d) -> t h d", d=HD),
                 )
@@ -200,6 +201,9 @@ def tile_transformerblock_pa_k_kernel(
                 quantise(c, h_by_t_of[c])
                 for g in range(c * X_CHUNK_GROUPS, (c + 1) * X_CHUNK_GROUPS):
                     project(g, 0, QK_COLS)
+
+        for g in range(GROUPS):
+            project(g, QK_COLS, V_COLS)
 
         cos_cos = keep.tile([P, 2, HALF], F32)
         nc.vector.tensor_copy(out=cos_cos[:], in_=rope_raw[:, 0:1, :].to_broadcast([P, 2, HALF]))
@@ -230,7 +234,7 @@ def tile_transformerblock_pa_k_kernel(
                     in1=sin_sin[:, half : half + 1, :].to_broadcast([P, HEADS_PER_BANK, HALF]),
                     op=ALU.mult,
                 )
-            rotated = finish.tile([P, BANK], F32)
+            rotated = finish.tile([P, BANK], F32, bufs=QK_BANKS)
             nc.vector.tensor_tensor(
                 out=rotated[:],
                 in0=straight[:].rearrange("p h s d -> p (h s d)"),
@@ -238,14 +242,12 @@ def tile_transformerblock_pa_k_kernel(
                 op=ALU.add,
             )
             out_tensor = out_0 if bank < QK_BANKS // 2 else out_1
-            store(rotated, out_tensor, (bank % 2) * HEADS_PER_BANK, nc.scalar)
+            store(rotated, out_tensor, (bank % 2) * HEADS_PER_BANK)
 
-        for g in range(GROUPS):
-            project(g, QK_COLS, V_COLS)
         for j in range(V_BANKS):
             bank = QK_BANKS + j
             value = finish.tile([P, BANK], F32)
             nc.vector.tensor_tensor(
                 out=value[:], in0=acc[bank][:], in1=bias_all[:, bank * BANK : (bank + 1) * BANK], op=ALU.add
             )
-            store(value, out_2, j * HEADS_PER_BANK, nc.sync)
+            store(value, out_2, j * HEADS_PER_BANK)

@@ -61,8 +61,8 @@ def tile_transformerblock_pa_k_kernel(
         nc.scalar.dma_start(out=bias_row[0:1, :], in_=b_qkv.rearrange("(o n) -> o n", o=1))
         rope_raw = keep.tile([P, 2, HALF], BF16)
         for b in range(2):
-            nc.scalar.dma_start(out=rope_raw[b * T : (b + 1) * T, 0, :], in_=rope_cos)
-            nc.scalar.dma_start(out=rope_raw[b * T : (b + 1) * T, 1, :], in_=rope_sin)
+            nc.scalar.dma_start(out=rope_raw[b:P:2, 0, :], in_=rope_cos)
+            nc.scalar.dma_start(out=rope_raw[b:P:2, 1, :], in_=rope_sin)
 
         x_chunks = []
         for c in range(X_CHUNKS):
@@ -85,6 +85,11 @@ def tile_transformerblock_pa_k_kernel(
 
         ident = keep.tile([P, P], F32)
         make_identity(nc, ident[:])
+        interleave = keep.tile([P, P], F32)
+        nc.vector.tensor_copy(
+            out=interleave[:].rearrange("p (t b) -> p b t", b=2),
+            in_=ident[:].rearrange("p (b t) -> p b t", b=2),
+        )
         ones = keep.tile([P, P], BF16)
         nc.vector.memset(ones[:], 1.0)
         eps = keep.tile([P, 1], F32)
@@ -140,7 +145,7 @@ def tile_transformerblock_pa_k_kernel(
                 g = c * X_CHUNK_GROUPS + i
                 flipped = psum_work.tile([P, PACK, P], F32, tag="work")
                 for t in range(PACK):
-                    nc.tensor.transpose(flipped[:, t, :], normed[:, i, t, :], ident[:])
+                    nc.tensor.transpose(flipped[:, t, :], normed[:, i, t, :], interleave[:])
                 for t in range(PACK):
                     nc.scalar.activation(
                         out=h_by_t[:, i, t, :],
@@ -186,7 +191,7 @@ def tile_transformerblock_pa_k_kernel(
             for b in range(2):
                 nc.sync.dma_start(
                     out=out_tensor[b, first_head : first_head + HEADS_PER_BANK].rearrange("h t d -> t h d"),
-                    in_=result[b * T : (b + 1) * T, :].rearrange("t (h d) -> t h d", d=HD),
+                    in_=result[b:P:2, :].rearrange("t (h d) -> t h d", d=HD),
                 )
 
         normed_of = {}

@@ -50,6 +50,9 @@ def tile_transformerblock_pa_k_kernel(
         psum_work = ctx.enter_context(tc.psum_pool(name="psum_work", bufs=2))
         ctx.enter_context(tc.manual_schedule())
 
+        ident = keep.tile([P, P], F32)
+        make_identity(nc, ident[:])
+
         gain_rows = keep.tile([P, K_PASS], BF16)
         nc.vector.memset(gain_rows[:], 0.0)
         nc.scalar.dma_start(out=gain_rows[0:GROUPS, :], in_=ln1_g.rearrange("(g k) -> g k", k=K_PASS))
@@ -83,8 +86,6 @@ def tile_transformerblock_pa_k_kernel(
                     ].bitcast(F32),
                 )
 
-        ident = keep.tile([P, P], F32)
-        make_identity(nc, ident[:])
         interleave = keep.tile([P, P], F32)
         nc.vector.tensor_copy(
             out=interleave[:].rearrange("p (t b) -> p b t", b=2),

@@ -29,6 +29,7 @@ V_BANKS = V_COLS // BANK
 X_CHUNK_GROUPS = 4
 X_CHUNK = X_CHUNK_GROUPS * K_PASS
 X_CHUNKS = D // X_CHUNK
+LEAD = 6
 PLANES_PER_TILE = 4
 EPS = 1e-5
 
@@ -140,22 +141,19 @@ def tile_transformerblock_pa_k_kernel(
             )
             return normed
 
-        def flip(c, normed):
-            h_by_t = stage.tile([P, X_CHUNK_GROUPS, PACK, P], BF16)
-            for i in range(X_CHUNK_GROUPS):
-                g = c * X_CHUNK_GROUPS + i
-                flipped = psum_work.tile([P, PACK, P], F32, tag="work")
-                for t in range(PACK):
-                    nc.tensor.transpose(flipped[:, t, :], normed[:, i, t, :], interleave[:])
-                for t in range(PACK):
-                    nc.scalar.activation(
-                        out=h_by_t[:, i, t, :],
-                        in_=flipped[:, t, :],
-                        func=ACT.Identity,
-                        scale=gain_cols[:, t, g : g + 1],
-                        bias=gain_cols[:, t, GROUPS + g : GROUPS + g + 1],
-                    )
-            return h_by_t
+        def flip(g, normed, h_by_t):
+            i = g % X_CHUNK_GROUPS
+            flipped = psum_work.tile([P, PACK, P], F32, tag="work")
+            for t in range(PACK):
+                nc.tensor.transpose(flipped[:, t, :], normed[:, i, t, :], interleave[:])
+            for t in range(PACK):
+                nc.scalar.activation(
+                    out=h_by_t[:, i, t, :],
+                    in_=flipped[:, t, :],
+                    func=ACT.Identity,
+                    scale=gain_cols[:, t, g : g + 1],
+                    bias=gain_cols[:, t, GROUPS + g : GROUPS + g + 1],
+                )
 
         def quantise(c, h_by_t):
             grouped = stage.tile([P, X_CHUNK_GROUPS, P, PACK], BF16, align_bytes=64)
@@ -197,16 +195,29 @@ def tile_transformerblock_pa_k_kernel(
 
         normed_of = {}
         h_by_t_of = {}
-        for step in range(X_CHUNKS + 2):
-            if step < X_CHUNKS:
-                normed_of[step] = normalise(step)
-            if 1 <= step <= X_CHUNKS:
-                h_by_t_of[step - 1] = flip(step - 1, normed_of[step - 1])
-            if step >= 2:
-                c = step - 2
+
+        def start(c):
+            normed_of[c] = normalise(c)
+
+        def turn(g):
+            c, i = divmod(g, X_CHUNK_GROUPS)
+            if i == 0:
+                h_by_t_of[c] = stage.tile([P, X_CHUNK_GROUPS, PACK, P], BF16, name="h_by_t")
+            flip(g, normed_of[c], h_by_t_of[c])
+
+        start(0)
+        start(1)
+        for g in range(LEAD):
+            turn(g)
+        for g in range(GROUPS):
+            c, i = divmod(g, X_CHUNK_GROUPS)
+            if i == 0:
                 quantise(c, h_by_t_of[c])
-                for g in range(c * X_CHUNK_GROUPS, (c + 1) * X_CHUNK_GROUPS):
-                    project(g, 0, QK_COLS)
+                if c + 2 < X_CHUNKS:
+                    start(c + 2)
+            if g + LEAD < GROUPS:
+                turn(g + LEAD)
+            project(g, 0, QK_COLS)
 
         for g in range(GROUPS):
             project(g, QK_COLS, V_COLS)

@@ -30,6 +30,7 @@ X_CHUNK_GROUPS = 4
 X_CHUNK = X_CHUNK_GROUPS * K_PASS
 X_CHUNKS = D // X_CHUNK
 LEAD = 6
+DMA_ALIGN = 512
 PLANES_PER_TILE = 4
 EPS = 1e-5
 
@@ -70,11 +71,11 @@ def tile_transformerblock_pa_k_kernel(
 
         x_chunks = []
         for c in range(X_CHUNKS):
-            x_chunk = keep.tile([P, X_CHUNK], BF16, name="x_chunk%d" % c)
+            x_chunk = keep.tile([P, X_CHUNK], BF16, name="x_chunk%d" % c, align_bytes=DMA_ALIGN)
             nc.sync.dma_start(out=x_chunk[:], in_=x_rows[:, c * X_CHUNK : (c + 1) * X_CHUNK])
             x_chunks.append(x_chunk)
 
-        w_planes = keep.tile([P, GROUPS // PLANES_PER_TILE, N_ALL], U8, align_bytes=64)
+        w_planes = keep.tile([P, GROUPS // PLANES_PER_TILE, N_ALL], U8, align_bytes=DMA_ALIGN)
         nc.vector.memset(w_planes[:].bitcast(I32), 0)
         for s in range(GROUPS // PLANES_PER_TILE):
             for quadrant in range(4):
@@ -166,7 +167,7 @@ def tile_transformerblock_pa_k_kernel(
             )
 
         def project(g, first_col, n_cols):
-            w_words = weights.tile([P, n_cols], I32, tag="w", align_bytes=64)
+            w_words = weights.tile([P, n_cols], I32, tag="w", align_bytes=DMA_ALIGN)
             nc.sync.dma_start(
                 out=w_words[:],
                 in_=w_qkv_words[g]
@@ -251,7 +252,7 @@ def tile_transformerblock_pa_k_kernel(
                     in1=sin_sin[:, half : half + 1, :].to_broadcast([P, HEADS_PER_BANK, HALF]),
                     op=ALU.mult,
                 )
-            rotated = finish.tile([P, BANK], F32, bufs=QK_BANKS)
+            rotated = finish.tile([P, BANK], F32, bufs=QK_BANKS, align_bytes=DMA_ALIGN)
             nc.vector.tensor_tensor(
                 out=rotated[:],
                 in0=straight[:].rearrange("p h s d -> p (h s d)"),
@@ -263,7 +264,7 @@ def tile_transformerblock_pa_k_kernel(
 
         for j in range(V_BANKS):
             bank = QK_BANKS + j
-            value = finish.tile([P, BANK], F32)
+            value = finish.tile([P, BANK], F32, align_bytes=DMA_ALIGN)
             nc.vector.tensor_tensor(
                 out=value[:], in0=acc[bank][:], in1=bias_all[:, bank * BANK : (bank + 1) * BANK], op=ALU.add
             )

@@ -30,6 +30,7 @@ X_CHUNK_GROUPS = 4
 X_CHUNK = X_CHUNK_GROUPS * K_PASS
 X_CHUNKS = D // X_CHUNK
 LEAD = 6
+WHOLE_GROUPS = 6
 DMA_ALIGN = 512
 PLANES_PER_TILE = 4
 EPS = 1e-5
@@ -46,7 +47,7 @@ def tile_transformerblock_pa_k_kernel(
     with ExitStack() as ctx:
         keep = ctx.enter_context(tc.tile_pool(name="keep", bufs=1))
         stage = ctx.enter_context(tc.tile_pool(name="stage", bufs=2))
-        weights = ctx.enter_context(tc.tile_pool(name="weights", bufs=12))
+        weights = ctx.enter_context(tc.tile_pool(name="weights", bufs=9))
         finish = ctx.enter_context(tc.tile_pool(name="finish", bufs=2))
         psum_acc = ctx.enter_context(tc.psum_pool(name="psum_acc", bufs=1))
         psum_work = ctx.enter_context(tc.psum_pool(name="psum_work", bufs=2))
@@ -126,8 +127,8 @@ def tile_transformerblock_pa_k_kernel(
         rstd = keep.tile([P, 1], F32)
         nc.vector.reciprocal(out=rstd[:], in_=std[:])
 
-        h_codes = keep.tile([P, GROUPS * P], I32, align_bytes=64)
-        h_planes = keep.tile([P, GROUPS * P], U8, align_bytes=64)
+        h_codes = keep.tile([P, GROUPS * P], I32, align_bytes=DMA_ALIGN)
+        h_planes = keep.tile([P, GROUPS * P], U8, align_bytes=DMA_ALIGN)
         acc = [psum_acc.tile([P, BANK], F32, name="acc%d" % j) for j in range(QK_BANKS + V_BANKS)]
 
         def normalise(c):
@@ -157,7 +158,7 @@ def tile_transformerblock_pa_k_kernel(
                 )
 
         def quantise(c, h_by_t):
-            grouped = stage.tile([P, X_CHUNK_GROUPS, P, PACK], BF16, align_bytes=64)
+            grouped = stage.tile([P, X_CHUNK_GROUPS, P, PACK], BF16, align_bytes=DMA_ALIGN)
             nc.vector.tensor_copy(out=grouped[:], in_=h_by_t[:].rearrange("p g t r -> p g r t"))
             words = slice(c * X_CHUNK_GROUPS * P, (c + 1) * X_CHUNK_GROUPS * P)
             nc.vector.quantize_mx(
@@ -218,9 +219,9 @@ def tile_transformerblock_pa_k_kernel(
                     start(c + 2)
             if g + LEAD < GROUPS:
                 turn(g + LEAD)
-            project(g, 0, QK_COLS)
+            project(g, 0, N_ALL if g < WHOLE_GROUPS else QK_COLS)
 
-        for g in range(GROUPS):
+        for g in range(WHOLE_GROUPS, GROUPS):
             project(g, QK_COLS, V_COLS)
 
         cos_cos = keep.tile([P, 2, HALF], F32)
@@ -231,36 +232,44 @@ def tile_transformerblock_pa_k_kernel(
         )
         nc.vector.tensor_copy(out=sin_sin[:, 1, :], in_=rope_raw[:, 1, :])
 
-        for bank in range(QK_BANKS):
-            cols = slice(bank * BANK, (bank + 1) * BANK)
-            biased = finish.tile([P, HEADS_PER_BANK, 2, HALF], F32)
-            nc.vector.tensor_tensor(
-                out=biased[:].rearrange("p h s d -> p (h s d)"), in0=acc[bank][:], in1=bias_all[:, cols], op=ALU.add
-            )
-            straight = finish.tile([P, HEADS_PER_BANK, 2, HALF], F32)
-            nc.vector.tensor_tensor(
-                out=straight[:].rearrange("p h s d -> p h (s d)"),
-                in0=biased[:].rearrange("p h s d -> p h (s d)"),
-                in1=cos_cos[:].rearrange("p s d -> p (s d)").unsqueeze(1).to_broadcast([P, HEADS_PER_BANK, HD]),
-                op=ALU.mult,
-            )
-            crossed = finish.tile([P, HEADS_PER_BANK, 2, HALF], F32)
-            for half in range(2):
+        for pair in range(0, QK_BANKS, 2):
+            banks = range(pair, pair + 2)
+            biased, straight, crossed = {}, {}, {}
+            for bank in banks:
+                biased[bank] = finish.tile([P, HEADS_PER_BANK, 2, HALF], F32, name="biased")
                 nc.vector.tensor_tensor(
-                    out=crossed[:, :, half, :],
-                    in0=biased[:, :, 1 - half, :],
-                    in1=sin_sin[:, half : half + 1, :].to_broadcast([P, HEADS_PER_BANK, HALF]),
+                    out=biased[bank][:].rearrange("p h s d -> p (h s d)"),
+                    in0=acc[bank][:],
+                    in1=bias_all[:, bank * BANK : (bank + 1) * BANK],
+                    op=ALU.add,
+                )
+            for bank in banks:
+                straight[bank] = finish.tile([P, HEADS_PER_BANK, 2, HALF], F32, name="straight")
+                nc.vector.tensor_tensor(
+                    out=straight[bank][:].rearrange("p h s d -> p h (s d)"),
+                    in0=biased[bank][:].rearrange("p h s d -> p h (s d)"),
+                    in1=cos_cos[:].rearrange("p s d -> p (s d)").unsqueeze(1).to_broadcast([P, HEADS_PER_BANK, HD]),
                     op=ALU.mult,
                 )
-            rotated = finish.tile([P, BANK], F32, bufs=QK_BANKS, align_bytes=DMA_ALIGN)
-            nc.vector.tensor_tensor(
-                out=rotated[:],
-                in0=straight[:].rearrange("p h s d -> p (h s d)"),
-                in1=crossed[:].rearrange("p h s d -> p (h s d)"),
-                op=ALU.add,
-            )
-            out_tensor = out_0 if bank < QK_BANKS // 2 else out_1
-            store(rotated, out_tensor, (bank % 2) * HEADS_PER_BANK)
+            for bank in banks:
+                crossed[bank] = finish.tile([P, HEADS_PER_BANK, 2, HALF], F32, name="crossed")
+                for half in range(2):
+                    nc.vector.tensor_tensor(
+                        out=crossed[bank][:, :, half, :],
+                        in0=biased[bank][:, :, 1 - half, :],
+                        in1=sin_sin[:, half : half + 1, :].to_broadcast([P, HEADS_PER_BANK, HALF]),
+                        op=ALU.mult,
+                    )
+            for bank in banks:
+                rotated = finish.tile([P, BANK], F32, name="rotated", bufs=QK_BANKS, align_bytes=DMA_ALIGN)
+                nc.vector.tensor_tensor(
+                    out=rotated[:],
+                    in0=straight[bank][:].rearrange("p h s d -> p (h s d)"),
+                    in1=crossed[bank][:].rearrange("p h s d -> p (h s d)"),
+                    op=ALU.add,
+                )
+                out_tensor = out_0 if bank < QK_BANKS // 2 else out_1
+                store(rotated, out_tensor, (bank % 2) * HEADS_PER_BANK)
 
         for j in range(V_BANKS):
             bank = QK_BANKS + j

from contextlib import ExitStack

import concourse.mybir as mybir
from concourse.masks import make_identity

F32 = mybir.dt.float32
BF16 = mybir.dt.bfloat16
I32 = mybir.dt.int32
U8 = mybir.dt.uint8
FP8X4 = mybir.dt.float8_e4m3fn_x4
ALU = mybir.AluOpType
ACT = mybir.ActivationFunctionType

P = 128
PACK = 4
K_PASS = P * PACK
D = 8192
GROUPS = D // K_PASS
BANK = 512
T = 64
HD = 64
HALF = HD // 2
HEADS_PER_BANK = BANK // HD
QK_COLS = 2048
V_COLS = 1024
N_ALL = QK_COLS + V_COLS
QK_BANKS = QK_COLS // BANK
V_BANKS = V_COLS // BANK
X_CHUNK_GROUPS = 4
X_CHUNK = X_CHUNK_GROUPS * K_PASS
X_CHUNKS = D // X_CHUNK
LEAD = 6
WHOLE_GROUPS = 6
DMA_ALIGN = 512
PLANES_PER_TILE = 4
EPS = 1e-5

FLOPS = 2 * P * D * N_ALL


def tile_transformerblock_pa_k_kernel(
    tc, x, rope_cos, rope_sin, ln1_g, ln1_b, w_qkv_words, w_qkv_scales, b_qkv, out_0, out_1, out_2
):
    nc = tc.nc
    x_rows = x.rearrange("b t d -> (b t) d")

    with ExitStack() as ctx:
        keep = ctx.enter_context(tc.tile_pool(name="keep", bufs=1))
        stage = ctx.enter_context(tc.tile_pool(name="stage", bufs=2))
        weights = ctx.enter_context(tc.tile_pool(name="weights", bufs=9))
        finish = ctx.enter_context(tc.tile_pool(name="finish", bufs=2))
        psum_acc = ctx.enter_context(tc.psum_pool(name="psum_acc", bufs=1))
        psum_work = ctx.enter_context(tc.psum_pool(name="psum_work", bufs=2))
        ctx.enter_context(tc.manual_schedule())

        ident = keep.tile([P, P], F32)
        make_identity(nc, ident[:])

        gain_rows = keep.tile([P, K_PASS], BF16)
        nc.vector.memset(gain_rows[:], 0.0)
        nc.scalar.dma_start(out=gain_rows[0:GROUPS, :], in_=ln1_g.rearrange("(g k) -> g k", k=K_PASS))
        nc.scalar.dma_start(
            out=gain_rows[GROUPS : 2 * GROUPS, :], in_=ln1_b.rearrange("(g k) -> g k", k=K_PASS)
        )
        bias_row = keep.tile([P, N_ALL], BF16)
        nc.vector.memset(bias_row[:], 0.0)
        nc.scalar.dma_start(out=bias_row[0:1, :], in_=b_qkv.rearrange("(o n) -> o n", o=1))
        rope_raw = keep.tile([P, 2, HALF], BF16)
        for b in range(2):
            nc.scalar.dma_start(out=rope_raw[b:P:2, 0, :], in_=rope_cos)
            nc.scalar.dma_start(out=rope_raw[b:P:2, 1, :], in_=rope_sin)

        x_chunks = []
        for c in range(X_CHUNKS):
            x_chunk = keep.tile([P, X_CHUNK], BF16, name="x_chunk%d" % c, align_bytes=DMA_ALIGN)
            nc.sync.dma_start(out=x_chunk[:], in_=x_rows[:, c * X_CHUNK : (c + 1) * X_CHUNK])
            x_chunks.append(x_chunk)

        w_planes = keep.tile([P, GROUPS // PLANES_PER_TILE, N_ALL], U8, align_bytes=DMA_ALIGN)
        nc.vector.memset(w_planes[:].bitcast(I32), 0)
        for s in range(GROUPS // PLANES_PER_TILE):
            for quadrant in range(4):
                nc.gpsimd.dma_start(
                    out=w_planes[32 * quadrant : 32 * quadrant + 16, s, :].bitcast(F32),
                    in_=w_qkv_scales[
                        PLANES_PER_TILE * s : PLANES_PER_TILE * (s + 1),
                        4 * quadrant : 4 * quadrant + 4,
                        :,
                    ].bitcast(F32),
                )

        interleave = keep.tile([P, P], F32)
        nc.vector.tensor_copy(
            out=interleave[:].rearrange("p (t b) -> p b t", b=2),
            in_=ident[:].rearrange("p (b t) -> p b t", b=2),
        )
        ones = keep.tile([P, P], BF16)
        nc.vector.memset(ones[:], 1.0)
        eps = keep.tile([P, 1], F32)
        nc.vector.memset(eps[:], EPS)
        table_warm = keep.tile([P, 1], F32)
        nc.scalar.activation(out=table_warm[:], in_=eps[:], func=ACT.Sqrt)

        bias_all = keep.tile([P, N_ALL], F32)
        for j in range(N_ALL // BANK):
            cols = slice(j * BANK, (j + 1) * BANK)
            spread = psum_work.tile([P, BANK], F32, tag="work")
            nc.tensor.matmul(out=spread[:], lhsT=ones[:], rhs=bias_row[:, cols], start=True, stop=True)
            nc.scalar.copy(out=bias_all[:, cols], in_=spread[:])

        gain_sorted = keep.tile([P, PACK, P], F32)
        nc.vector.tensor_copy(out=gain_sorted[:], in_=gain_rows[:].rearrange("r (p t) -> r t p", t=PACK))
        gain_t = psum_work.tile([P, PACK, P], F32, tag="work")
        for t in range(PACK):
            nc.tensor.transpose(gain_t[:, t, :], gain_sorted[:, t, :], ident[:])
        gain_cols = keep.tile([P, PACK, 2 * GROUPS], F32)
        nc.scalar.copy(out=gain_cols[:], in_=gain_t[:, :, 0 : 2 * GROUPS])

        stats = keep.tile([P, GROUPS, 6], F32)
        for g in range(GROUPS):
            c, i = divmod(g, X_CHUNK_GROUPS)
            nc.vector.bn_stats(out=stats[:, g, :], in_=x_chunks[c][:, i * K_PASS : (i + 1) * K_PASS])
        mean_var = keep.tile([P, 2], F32)
        nc.vector.bn_aggr(out=mean_var[:], in_=stats[:].rearrange("p g s -> p (g s)"))
        std = keep.tile([P, 1], F32)
        nc.scalar.activation(out=std[:], in_=mean_var[:, 1:2], func=ACT.Sqrt, bias=eps[:], scale=1.0)
        rstd = keep.tile([P, 1], F32)
        nc.vector.reciprocal(out=rstd[:], in_=std[:])

        h_codes = keep.tile([P, GROUPS * P], I32, align_bytes=DMA_ALIGN)
        h_planes = keep.tile([P, GROUPS * P], U8, align_bytes=DMA_ALIGN)
        acc = [psum_acc.tile([P, BANK], F32, name="acc%d" % j) for j in range(QK_BANKS + V_BANKS)]

        def normalise(c):
            normed = stage.tile([P, X_CHUNK_GROUPS, PACK, P], F32, bufs=3)
            nc.vector.tensor_scalar(
                out=normed[:],
                in0=x_chunks[c][:].rearrange("r (g p t) -> r g t p", g=X_CHUNK_GROUPS, t=PACK),
                scalar1=mean_var[:, 0:1],
                scalar2=rstd[:],
                op0=ALU.subtract,
                op1=ALU.mult,
            )
            return normed

        def flip(g, normed, h_by_t):
            i = g % X_CHUNK_GROUPS
            flipped = psum_work.tile([P, PACK, P], F32, tag="work")
            for t in range(PACK):
                nc.tensor.transpose(flipped[:, t, :], normed[:, i, t, :], interleave[:])
            for t in range(PACK):
                nc.scalar.activation(
                    out=h_by_t[:, i, t, :],
                    in_=flipped[:, t, :],
                    func=ACT.Identity,
                    scale=gain_cols[:, t, g : g + 1],
                    bias=gain_cols[:, t, GROUPS + g : GROUPS + g + 1],
                )

        def quantise(c, h_by_t):
            grouped = stage.tile([P, X_CHUNK_GROUPS, P, PACK], BF16, align_bytes=DMA_ALIGN)
            nc.vector.tensor_copy(out=grouped[:], in_=h_by_t[:].rearrange("p g t r -> p g r t"))
            words = slice(c * X_CHUNK_GROUPS * P, (c + 1) * X_CHUNK_GROUPS * P)
            nc.vector.quantize_mx(
                out=h_codes[:, words].bitcast(FP8X4),
                scales=h_planes[:, words],
                in_=grouped[:].rearrange("p g r t -> p (g r t)"),
            )

        def project(g, first_col, n_cols):
            w_words = weights.tile([P, n_cols], I32, tag="w", align_bytes=DMA_ALIGN)
            nc.sync.dma_start(
                out=w_words[:],
                in_=w_qkv_words[g]
                .rearrange("p n t -> p (n t)")[:, first_col * PACK : (first_col + n_cols) * PACK]
                .bitcast(I32),
            )
            s, plane = divmod(g, PLANES_PER_TILE)
            for j in range(n_cols // BANK):
                bank = first_col // BANK + j
                nc.tensor.matmul_mx(
                    out=acc[bank][:],
                    lhsT=h_codes[:, g * P : (g + 1) * P].bitcast(FP8X4),
                    lhsT_scale=h_planes[:, g * P : (g + 1) * P],
                    rhs=w_words[:, j * BANK : (j + 1) * BANK].bitcast(FP8X4),
                    rhs_scale=w_planes[4 * plane : P, s, bank * BANK : (bank + 1) * BANK],
                    start=(g == 0),
                    stop=(g == GROUPS - 1),
                )

        def store(result, out_tensor, first_head):
            for b in range(2):
                nc.sync.dma_start(
                    out=out_tensor[b, first_head : first_head + HEADS_PER_BANK].rearrange("h t d -> t h d"),
                    in_=result[b:P:2, :].rearrange("t (h d) -> t h d", d=HD),
                )

        normed_of = {}
        h_by_t_of = {}

        def start(c):
            normed_of[c] = normalise(c)

        def turn(g):
            c, i = divmod(g, X_CHUNK_GROUPS)
            if i == 0:
                h_by_t_of[c] = stage.tile([P, X_CHUNK_GROUPS, PACK, P], BF16, name="h_by_t")
            flip(g, normed_of[c], h_by_t_of[c])

        start(0)
        start(1)
        for g in range(LEAD):
            turn(g)
        for g in range(GROUPS):
            c, i = divmod(g, X_CHUNK_GROUPS)
            if i == 0:
                quantise(c, h_by_t_of[c])
                if c + 2 < X_CHUNKS:
                    start(c + 2)
            if g + LEAD < GROUPS:
                turn(g + LEAD)
            project(g, 0, N_ALL if g < WHOLE_GROUPS else QK_COLS)

        for g in range(WHOLE_GROUPS, GROUPS):
            project(g, QK_COLS, V_COLS)

        cos_cos = keep.tile([P, 2, HALF], F32)
        nc.vector.tensor_copy(out=cos_cos[:], in_=rope_raw[:, 0:1, :].to_broadcast([P, 2, HALF]))
        sin_sin = keep.tile([P, 2, HALF], F32)
        nc.vector.tensor_scalar(
            out=sin_sin[:, 0, :], in0=rope_raw[:, 1, :], scalar1=-1.0, scalar2=None, op0=ALU.mult
        )
        nc.vector.tensor_copy(out=sin_sin[:, 1, :], in_=rope_raw[:, 1, :])

        for pair in range(0, QK_BANKS, 2):
            banks = range(pair, pair + 2)
            biased, straight, crossed = {}, {}, {}
            for bank in banks:
                biased[bank] = finish.tile([P, HEADS_PER_BANK, 2, HALF], F32, name="biased")
                nc.vector.tensor_tensor(
                    out=biased[bank][:].rearrange("p h s d -> p (h s d)"),
                    in0=acc[bank][:],
                    in1=bias_all[:, bank * BANK : (bank + 1) * BANK],
                    op=ALU.add,
                )
            for bank in banks:
                straight[bank] = finish.tile([P, HEADS_PER_BANK, 2, HALF], F32, name="straight")
                nc.vector.tensor_tensor(
                    out=straight[bank][:].rearrange("p h s d -> p h (s d)"),
                    in0=biased[bank][:].rearrange("p h s d -> p h (s d)"),
                    in1=cos_cos[:].rearrange("p s d -> p (s d)").unsqueeze(1).to_broadcast([P, HEADS_PER_BANK, HD]),
                    op=ALU.mult,
                )
            for bank in banks:
                crossed[bank] = finish.tile([P, HEADS_PER_BANK, 2, HALF], F32, name="crossed")
                for half in range(2):
                    nc.vector.tensor_tensor(
                        out=crossed[bank][:, :, half, :],
                        in0=biased[bank][:, :, 1 - half, :],
                        in1=sin_sin[:, half : half + 1, :].to_broadcast([P, HEADS_PER_BANK, HALF]),
                        op=ALU.mult,
                    )
            for bank in banks:
                rotated = finish.tile([P, BANK], F32, name="rotated", bufs=QK_BANKS, align_bytes=DMA_ALIGN)
                nc.vector.tensor_tensor(
                    out=rotated[:],
                    in0=straight[bank][:].rearrange("p h s d -> p (h s d)"),
                    in1=crossed[bank][:].rearrange("p h s d -> p (h s d)"),
                    op=ALU.add,
                )
                out_tensor = out_0 if bank < QK_BANKS // 2 else out_1
                store(rotated, out_tensor, (bank % 2) * HEADS_PER_BANK)

        for j in range(V_BANKS):
            bank = QK_BANKS + j
            value = finish.tile([P, BANK], F32, align_bytes=DMA_ALIGN)
            nc.vector.tensor_tensor(
                out=value[:], in0=acc[bank][:], in1=bias_all[:, bank * BANK : (bank + 1) * BANK], op=ALU.add
            )
            store(value, out_2, j * HEADS_PER_BANK)
